import numpy as np
import ml_dtypes


def mxq(x, axis, fmt="e4m3"):
    dtype, down = {"e4m3": (ml_dtypes.float8_e4m3fn, 7), "e5m2": (ml_dtypes.float8_e5m2, 14)}[fmt]
    v = np.moveaxis(np.asarray(x, np.float32).astype(ml_dtypes.bfloat16).astype(np.float64), axis, -1)
    blocks = v.reshape(v.shape[:-1] + (-1, 32))
    amax = np.abs(blocks).max(-1, keepdims=True)
    byte = np.maximum(np.where(amax > 0, np.frexp(amax)[1] - 1 + 127, 0) - down, 1)
    scale = np.exp2(byte - 127.0)
    codes = (blocks / scale).astype(np.float32).astype(dtype).astype(np.float64)
    return np.moveaxis((codes * scale).reshape(v.shape), -1, axis)


WIDE = False


def mx_kscale(k):
    if not WIDE:
        return np.ones(k)
    levels = np.array([10, -10, 5, -5, 0])
    if k % 512:
        return np.exp2(np.random.permutation(np.resize(levels, k // 32))).repeat(32)
    a = np.empty((k // 512, 16))
    for p in range(k // 512):
        a[p, :8] = np.random.permutation(np.resize(levels, 8))
        for g in range(8):
            far = levels[np.abs(levels - a[p, g]) >= 10]
            a[p, g + 8] = far[np.random.randint(len(far))]
    return np.exp2(a.ravel()).repeat(32)


BF16 = ml_dtypes.bfloat16


def bf(x):
    return np.asarray(x, np.float32).astype(BF16)


def f64(x):
    return np.asarray(x).astype(np.float64)


B, H, W, DIM, NH, HD, WH, WW = 8, 16, 16, 512, 16, 32, 8, 8
E = NH * HD
N = WH * WW
HALF = HD // 2


def cos_sin(n):
    inv_freq = 1.0 / (10000.0 ** (f64(np.arange(0, HALF, 2)) / HALF))
    ang = f64(np.arange(n))[:, None] * inv_freq
    return np.concatenate([np.cos(ang)] * 2, -1), np.concatenate([np.sin(ang)] * 2, -1)


def rot_half(u):
    u1, u2 = np.split(u, 2, axis=-1)
    return np.concatenate([-u2, u1], -1)


def rope2(t):
    cos_h, sin_h = cos_sin(WH)
    cos_w, sin_w = cos_sin(WW)
    th, tw = t[..., :HALF], t[..., HALF:]
    th = th * cos_h[:, None, :] + rot_half(th) * sin_h[:, None, :]
    tw = tw * cos_w[None, :, :] + rot_half(tw) * sin_w[None, :, :]
    return np.concatenate([th, tw], -1)


def draw0():
    s = mx_kscale(DIM)
    return {"x": bf(np.random.standard_normal((B, H, W, DIM)) * s),
            "qkv_w": bf(np.random.standard_normal((DIM, 3 * E)) / np.sqrt(DIM) / s[:, None]),
            "qkv_b": bf(np.random.standard_normal(3 * E) * 0.3)}


def core(x, qkv_w, qkv_b):
    xw = f64(x).reshape(B, H // WH, WH, W // WW, WW, DIM).transpose(0, 1, 3, 2, 4, 5).reshape(-1, N, DIM)
    BW = xw.shape[0]
    qkv = (mxq(xw, 2, "e4m3") @ mxq(f64(qkv_w), 0, "e4m3")) + f64(qkv_b)
    qkv = qkv.reshape(BW, N, 3, NH, HD).transpose(2, 0, 3, 1, 4)
    q, k, v = qkv[0], qkv[1], qkv[2]
    q = rope2(q.reshape(-1, WH, WW, HD)).reshape(BW, NH, N, HD)
    k = rope2(k.reshape(-1, WH, WW, HD)).reshape(BW, NH, N, HD)
    return q, k, np.ascontiguousarray(v)


def e4m3fn_bytes(y):
    return np.clip(np.asarray(y, np.float64), -448.0, 448.0).astype(np.float32).astype(ml_dtypes.float8_e4m3fn).view(np.uint8)


def e4m3fn_values(b):
    return np.asarray(b, np.uint8).view(ml_dtypes.float8_e4m3fn).astype(np.float64)


def setup_inputs():
    d = draw0()
    x0 = np.asarray(d['x']).astype(np.float64)
    s = (np.max(np.abs(x0), axis=(0, 1, 2), keepdims=True) / 448.0).astype(np.float32)
    out = {}
    for k, v in d.items():
        if k == 'x':
            out['x_bytes'] = e4m3fn_bytes(x0 / s.astype(np.float64))
            out['x_scale'] = s
        else:
            out[k] = v
    return out


def reference(x_bytes, x_scale, qkv_w, qkv_b):
    return core(e4m3fn_values(x_bytes) * x_scale.astype(np.float64), qkv_w, qkv_b)

@@ -1,0 +1,374 @@
+import math
+from contextlib import ExitStack
+
+import concourse.mybir as mybir
+from concourse.masks import make_identity
+
+FLOPS = 2 * 2048 * 512 * 1536
+
+F32 = mybir.dt.float32
+BF16 = mybir.dt.bfloat16
+U32 = mybir.dt.uint32
+U8 = mybir.dt.uint8
+FP8 = mybir.dt.float8_e4m3fn
+FP8X4 = mybir.dt.float8_e4m3fn_x4
+ALU = mybir.AluOpType
+ACTF = mybir.ActivationFunctionType
+AX = mybir.AxisListType
+
+P = 128
+NPOS = 8
+NFREQ = 8
+NH = 16
+HD = 32
+E = 512
+KDIM = 512
+CHUNK = 512
+
+UNITS = [(pq, rb, ch) for rb in range(2) for ch in range(2) for pq in range(2)]
+NPAIR = 2 * len(UNITS)
+P_B_ON_V = frozenset((11, 15))
+EV_ON_V = frozenset(((7, 1), (7, 3)))
+V_AT = {0: ((0, 0), (0, 1)), 1: ((0, 2), (0, 3)), 4: ((0, 4), (0, 5)), 5: ((0, 6), (0, 7)), 7: ((1, 0), (1, 1)), 8: ((1, 2), (1, 3)), 10: ((1, 4), (1, 5)), 11: ((1, 6), (1, 7))}
+XDEQ_AT = {0: ((1, 0),), 1: ((1, 1),), 3: ((2, 0),), 4: ((2, 1),), 6: ((3, 0),), 7: ((3, 1),)}
+MX_LEAD = 1
+V_HALF = True
+HALF_FROM = 0
+
+
+def tile_hydra_attn_pa_kernel(tc, x_bytes, x_scale, qkv_w, qkv_b, out_0, out_1, out_2):
+    nc = tc.nc
+    outs = (out_0, out_1, out_2)
+
+    with ExitStack() as ctx:
+        const = ctx.enter_context(tc.tile_pool(name="const", bufs=1))
+        xwork = ctx.enter_context(tc.tile_pool(name="xwork", bufs=3))
+        wwork = ctx.enter_context(tc.tile_pool(name="wwork", bufs=2))
+        rot = ctx.enter_context(tc.tile_pool(name="rot", bufs=3))
+        psum = ctx.enter_context(tc.psum_pool(name="psum", bufs=8))
+        ctx.enter_context(tc.manual_schedule())
+
+        sc = const.tile([P, KDIM], F32, name="sc")
+        x_rows = x_bytes.rearrange("b (wi rp rb) (j c) k -> rb (b wi rp) j (c k)", wi=2, rp=4, rb=2, j=2)
+        w_rows = qkv_w.rearrange("(p t) n -> p t n", t=4)
+        xb = []
+        wraw = []
+        for T in range(4):
+            xb_T = const.tile([P, 4 * KDIM], U8, name="xb%d" % T)
+            xb.append(xb_T)
+        for part in range(3):
+            wraw_p = const.tile([P, 4, E], BF16, name="wraw%d" % part)
+            wraw.append(wraw_p)
+
+        def load_x(T):
+            nc.sync.dma_start(out=xb[T][:], in_=x_rows[T // 2, :, :, (T % 2) * 2048:(T % 2 + 1) * 2048])
+
+        def load_w(part):
+            nc.sync.dma_start(out=wraw[part][:], in_=w_rows[:, :, part * E:(part + 1) * E])
+
+        brow = const.tile([P, P], BF16, name="brow")
+        nc.vector.memset(brow[:], 0.0)
+        load_x(0)
+        nc.sync.dma_start(out=sc[:], in_=x_scale.rearrange("a b c k -> (a b c k)").partition_broadcast(P))
+        for q in range(2):
+            nc.sync.dma_start(
+                out=brow[q * 4:(q + 1) * 4, :].rearrange("p (h i) -> p h i", i=NFREQ),
+                in_=qkv_b[q * E:(q + 1) * E].rearrange("(h f i) -> f h i", h=NH, f=4, i=NFREQ),
+            )
+        load_w(0)
+        load_w(1)
+        load_w(2)
+        bv = const.tile([P, E], BF16, name="bv")
+        nc.sync.dma_start(out=bv[:], in_=qkv_b[2 * E:3 * E].partition_broadcast(P))
+        load_x(1)
+        load_x(2)
+        load_x(3)
+
+        ident = const.tile([P, P], F32, name="ident")
+        make_identity(nc, ident[:])
+        zo = const.tile([P, 2], F32, name="zo")
+        nc.vector.memset(zo[:, 0:1], 0.0)
+        nc.vector.memset(zo[:, 1:2], 1.0)
+        tab = const.tile([P, 2, NPOS, NFREQ], F32, name="tab")
+        nc.vector.memset(tab[:, 0, 0, :], 1.0)
+        nc.vector.memset(tab[:, 1, 0, :], 0.0)
+        for pos in range(1, NPOS):
+            for s in range(2):
+                for i in range(0, NFREQ, 2):
+                    ang = (pos * 10000.0 ** (-i / 8.0), pos * 10000.0 ** (-(i + 1) / 8.0))
+                    va = math.cos(ang[0]) if s == 0 else math.sin(ang[0])
+                    vb = math.cos(ang[1]) if s == 0 else math.sin(ang[1])
+                    dst = tab[:, s, pos, i:i + 2]
+                    if s == 0:
+                        nc.vector.tensor_scalar(out=dst, in0=zo[:], scalar1=vb - va, scalar2=va, op0=ALU.mult,
+                                                op1=ALU.add)
+                    else:
+                        nc.scalar.activation(out=dst, in_=zo[:], func=ACTF.Copy, bias=va, scale=vb - va)
+        perm = const.tile([P, P], F32, name="perm")
+        nc.vector.tensor_copy(out=perm[:].rearrange("p (b j r) -> p b j r", b=16, j=2, r=4),
+                              in_=ident[:].rearrange("p (b r j) -> p b j r", b=16, r=4, j=2))
+        pick = const.tile([P, NFREQ], F32, name="pick")
+        nc.vector.tensor_reduce(out=pick[:], in_=ident[:].rearrange("p (h i) -> p i h", i=NFREQ), axis=AX.X, op=ALU.add)
+        tabm = const.tile([P, 2 * NPOS, NFREQ], F32, name="tabm")
+        nc.vector.tensor_tensor(out=tabm[:], in0=tab[:].rearrange("p s q i -> p (s q) i"),
+                                in1=pick[:].unsqueeze(1).to_broadcast([P, 2 * NPOS, NFREQ]), op=ALU.mult)
+        cs = const.tile([P, 3 * NPOS], F32, name="cs")
+        nc.vector.tensor_reduce(out=cs[:, 0:2 * NPOS], in_=tabm[:], axis=AX.X, op=ALU.add)
+        nc.vector.tensor_scalar(out=cs[:, 2 * NPOS:3 * NPOS], in0=cs[:, NPOS:2 * NPOS], scalar1=-1.0, scalar2=None,
+                                op0=ALU.mult)
+        xc = []
+        xs = []
+        for T in range(4):
+            xc_T = const.tile([P, CHUNK], U32, name="xc%d" % T, align_bytes=64)
+            xs_T = const.tile([P, CHUNK], U8, name="xs%d" % T, align_bytes=64)
+            xc.append(xc_T)
+            xs.append(xs_T)
+
+        def x_widen(T, a2):
+            xt = psum.tile([P, 512], F32, name="xt", tag="bank")
+            for a in range(2):
+                t4 = 2 * a2 + a
+                xq = xwork.tile([P, KDIM], BF16, name="xq", bufs=4)
+                nc.vector.tensor_tensor(out=xq[:], in0=xb[T][:, t4 * KDIM:(t4 + 1) * KDIM].bitcast(FP8),
+                                        in1=sc[:], op=ALU.mult)
+                words = xq[:].bitcast(F32)
+                for u in range(2):
+                    nc.tensor.transpose(xt[:, (2 * a + u) * P:(2 * a + u + 1) * P], words[:, u:256:2], perm[:])
+            return xt
+
+        def x_copy(xt):
+            xg = xwork.tile([P, 1024], BF16, name="xg", align_bytes=64)
+            nc.scalar.copy(out=xg[:].bitcast(F32).rearrange("p (a m u) -> p a m u", a=2, u=2),
+                           in_=xt[:].rearrange("p (a u m) -> p a m u", a=2, u=2))
+            return xg
+
+        def x_quant(T, a2, xg):
+            nc.vector.quantize_mx(out=xc[T][:, a2 * 256:(a2 + 1) * 256].bitcast(FP8X4),
+                                  scales=xs[T][:, a2 * 256:(a2 + 1) * 256], in_=xg[:])
+
+        wc = []
+        ws = []
+        for part in range(3):
+            wc_p = const.tile([P, E], U32, name="wc%d" % part, align_bytes=64)
+            ws_p = const.tile([P, E], U8, name="ws%d" % part, align_bytes=64)
+            wc.append(wc_p)
+            ws.append(ws_p)
+
+        def w_lace_qk(part, g, on_act):
+            wg = wwork.tile([P, 2 * E], BF16, name="wgh", bufs=4, align_bytes=64)
+            src = wraw[part][:].rearrange("p t (h x) -> p h x t", x=HD)
+            for half in range(2):
+                f = 2 * g + half
+                dst = wg[:, half * 512:(half + 1) * 512].rearrange("p (h i t) -> p h i t", h=NH, i=NFREQ, t=4)
+                if on_act:
+                    nc.scalar.copy(out=dst, in_=src[:, :, f * 8:(f + 1) * 8, :])
+                else:
+                    nc.gpsimd.tensor_scalar(out=dst, in0=src[:, :, f * 8:(f + 1) * 8, :], scalar1=1.0, scalar2=0.0,
+                                            op0=ALU.mult, op1=ALU.add)
+            return wg
+
+        def w_quant_qk(part, g, wg):
+            nc.vector.quantize_mx(out=wc[part][:, g * 256:(g + 1) * 256].bitcast(FP8X4),
+                                  scales=ws[part][:, g * 256:(g + 1) * 256], in_=wg[:])
+
+        def w_lace_v():
+            wg = wwork.tile([P, 4 * E], BF16, name="wg", bufs=1, align_bytes=64)
+            nc.vector.tensor_copy(out=wg[:].rearrange("p (n t) -> p n t", t=4), in_=wraw[2][:].rearrange("p t n -> p n t"))
+            return wg
+
+        def mx(out, lc, ls, rc, rs):
+            nc.tensor.matmul_mx(out=out, lhsT=lc.bitcast(FP8X4), lhsT_scale=ls, rhs=rc.bitcast(FP8X4), rhs_scale=rs,
+                                start=True, stop=True)
+
+        def pair_of(s):
+            pq, rbit, ch = UNITS[s // 2]
+            return pq, rbit, ch, 1 - s % 2
+
+        def mx_pair(s):
+            pq, rbit, ch, g = pair_of(s)
+            T = 2 * rbit + ch
+            y = []
+            for half in range(2):
+                f = 2 * g + half
+                y_h = psum.tile([P, 512], F32, name="y%d" % half, tag="bank")
+                mx(y_h[:], wc[pq][:, f * P:(f + 1) * P], ws[pq][:, f * P:(f + 1) * P], xc[T][:], xs[T][:])
+                y.append(y_h)
+            return y
+
+        def views(s):
+            pq, rbit, ch, g = pair_of(s)
+            if g == 1:
+                def yv(t, k):
+                    return t[:, k * P:(k + 1) * P]
+                return yv, yv, [4 * ch + k for k in range(4)]
+
+            def yr(t, k):
+                return t[:].rearrange("p (a w r) -> p r w a", a=4, w=32, r=4)[:, k]
+
+            def sr(t, k):
+                return t[:].rearrange("p (w r a) -> p r w a", w=32, r=4, a=4)[:, k]
+            return yr, sr, [2 * k + rbit for k in range(4)]
+
+        def first_products(s, y):
+            pq, rbit, ch, g = pair_of(s)
+            yv, sv, poss = views(s)
+            pt = []
+            ot = []
+            for half in range(2):
+                p_h = rot.tile([P, 512], F32, name="p%d%d" % (g, half))
+                o_h = rot.tile([P, 512], F32, name="o%d%d" % (g, half))
+                pt.append(p_h)
+                ot.append(o_h)
+            for half in range(2):
+                col = pq * 4 + 2 * g + half
+                for k in range(4):
+                    pos = poss[k]
+                    dst = sv(ot[half], k) if pos == 0 else sv(pt[half], k)
+                    if half == 1 and s in P_B_ON_V:
+                        nc.vector.tensor_scalar(out=dst, in0=yv(y[half], k), scalar1=cs[:, pos:pos + 1],
+                                                scalar2=rb[:, col, pos:pos + 1], op0=ALU.mult, op1=ALU.add)
+                    else:
+                        nc.scalar.activation(out=dst, in_=yv(y[half], k), func=ACTF.Identity,
+                                             bias=rb[:, col, pos:pos + 1], scale=cs[:, pos:pos + 1])
+            return pt, ot
+
+        def second_products(s, y, pt, ot):
+            yv, sv, poss = views(s)
+            for half in range(2):
+                soff = 2 * NPOS if half == 0 else NPOS
+                for k in range(4):
+                    pos = poss[k]
+                    if pos > 0:
+                        nc.vector.scalar_tensor_tensor(out=sv(ot[half], k), in0=yv(y[1 - half], k),
+                                                       scalar=cs[:, soff + pos:soff + pos + 1], in1=sv(pt[half], k),
+                                                       op0=ALU.mult, op1=ALU.add)
+
+        out_t = []
+        for part in range(3):
+            out_p = const.tile([P, NH, 2, NPOS, HD], F32, name="out%d" % part)
+            out_t.append(out_p)
+
+        def store(part, rbit, c0, c1):
+            dst = outs[part].rearrange("w h (rp rb c) d -> rp rb w h c d", rp=4, rb=2, c=8)
+            for rp in range(4):
+                nc.sync.dma_start(out=dst[rp, rbit, :, :, c0:c1, :].rearrange("w h c d -> w h (c d)"),
+                                  in_=out_t[part][rp:P:4, :, rbit, c0:c1, :].rearrange("p h c d -> p h (c d)"))
+
+        def turn_back(o0, o1, t4):
+            tr = psum.tile([P, 512], F32, name="tr", tag="bank")
+            for half in range(2):
+                nc.tensor.transpose(tr[:, half * P:(half + 1) * P], o0[half][:, t4:512:4], ident[:])
+            for half in range(2):
+                nc.tensor.transpose(tr[:, (2 + half) * P:(3 + half) * P], o1[half][:, t4 * P:(t4 + 1) * P], ident[:])
+            return tr
+
+        def copy_out(tr, u, t4):
+            pq, rbit, ch = UNITS[u]
+            dst = out_t[pq][:, :, rbit, 4 * ch + t4, :].rearrange("p h (f i) -> p h f i", f=4)
+            src = tr[:].rearrange("p (f h i) -> p h f i", f=4, h=NH, i=NFREQ)
+            if (u, t4) in EV_ON_V:
+                nc.vector.tensor_copy(out=dst, in_=src)
+            else:
+                nc.scalar.copy(out=dst, in_=src)
+
+        def v_mx(rbit, c):
+            T = 2 * rbit + c // 4
+            t4 = c % 4
+            yv_ = psum.tile([P, 512], F32, name="yv_", tag="bank")
+            mx(yv_[:], xc[T][:, t4 * P:(t4 + 1) * P], xs[T][:, t4 * P:(t4 + 1) * P], wc[2][:], ws[2][:])
+            return yv_
+
+        def v_add(yv_, rbit, c):
+            nc.vector.tensor_tensor(out=out_t[2][:, :, rbit, c, :], in0=yv_[:].rearrange("p (h d) -> p h d", d=HD),
+                                    in1=bv[:].rearrange("p (h d) -> p h d", d=HD), op=ALU.add)
+
+        wg_q1 = w_lace_qk(0, 1, False)
+        wg_k1 = w_lace_qk(1, 1, False)
+        wg_k0 = w_lace_qk(1, 0, False)
+        xt0 = x_widen(0, 0)
+        xt1 = x_widen(0, 1)
+        browf = const.tile([P, P], F32, name="browf")
+        nc.vector.tensor_copy(out=browf[:], in_=brow[:])
+        bps = psum.tile([P, 512], F32, name="bps", tag="bank")
+        nc.tensor.transpose(bps[:, 0:P], browf[:], ident[:])
+        bT = const.tile([P, 4, 2], F32, name="bT")
+        nc.vector.tensor_copy(out=bT[:].rearrange("p a b -> p (a b)"), in_=bps[:, 0:8])
+        bS = const.tile([P, 4, 2], F32, name="bS")
+        nc.vector.tensor_scalar(out=bS[:, :, 0], in0=bT[:, :, 1], scalar1=-1.0, scalar2=None, op0=ALU.mult)
+        nc.vector.tensor_copy(out=bS[:, :, 1], in_=bT[:, :, 0])
+        rb = const.tile([P, 8, NPOS], F32, name="rb")
+        rb2 = const.tile([P, 8, NPOS], F32, name="rb2")
+        nc.vector.tensor_tensor(out=rb2[:], in0=cs[:, 0:NPOS].unsqueeze(1).to_broadcast([P, 8, NPOS]),
+                                in1=bT[:].rearrange("p a b -> p (a b)").unsqueeze(2).to_broadcast([P, 8, NPOS]), op=ALU.mult)
+        nc.vector.tensor_tensor(out=rb[:], in0=cs[:, NPOS:2 * NPOS].unsqueeze(1).to_broadcast([P, 8, NPOS]),
+                                in1=bS[:].rearrange("p a b -> p (a b)").unsqueeze(2).to_broadcast([P, 8, NPOS]), op=ALU.mult)
+        nc.vector.tensor_tensor(out=rb[:], in0=rb[:], in1=rb2[:], op=ALU.add)
+
+        xg0 = x_copy(xt0)
+        xg1 = x_copy(xt1)
+        wg_q0 = w_lace_qk(0, 0, True)
+        x_quant(0, 0, xg0)
+        w_quant_qk(0, 1, wg_q1)
+        x_quant(0, 1, xg1)
+        w_quant_qk(0, 0, wg_q0)
+        ys = {}
+        ys[0] = mx_pair(0)
+        ys[1] = mx_pair(1)
+        mx_done = 2
+        wg_v = w_lace_v()
+        w_quant_qk(1, 1, wg_k1)
+        nc.vector.quantize_mx(out=wc[2][:].bitcast(FP8X4), scales=ws[2][:], in_=wg_v[:])
+        w_quant_qk(1, 0, wg_k0)
+        pend_copy = []
+        pend_quant = []
+        chunk_ready = {0: 2, 1: 0, 2: 0, 3: 0}
+        pend_v = []
+        v_count = {0: 0, 1: 0}
+        ps_ = {}
+        os_ = {}
+        k_quant = False
+
+        for s in range(NPAIR + 3):
+            if 1 <= s <= NPAIR:
+                second_products(s - 1, ys[s - 1], ps_[s - 1], os_[s - 1])
+            for rbit, c, yv_ in pend_v:
+                v_add(yv_, rbit, c)
+                v_count[rbit] += 1
+                if V_HALF and v_count[rbit] % 4 == 0:
+                    store(2, rbit, v_count[rbit] - 4, v_count[rbit])
+                elif v_count[rbit] == NPOS:
+                    store(2, rbit, 0, NPOS)
+            pend_v = []
+            trs = []
+            if s >= 3:
+                u = (s - 3) // 2
+                for t4 in ((0, 1) if (s - 3) % 2 == 0 else (2, 3)):
+                    trs.append((u, t4, turn_back(os_[2 * u + 1], os_[2 * u], t4)))
+            if s < NPAIR:
+                ps_[s], os_[s] = first_products(s, ys[s])
+            for T, a2, xg in pend_quant:
+                x_quant(T, a2, xg)
+                chunk_ready[T] += 1
+            pend_quant = []
+            while mx_done < NPAIR and mx_done <= s + MX_LEAD:
+                npq, nrb, nch, ng = pair_of(mx_done)
+                if chunk_ready[2 * nrb + nch] < 2:
+                    break
+                ys[mx_done] = mx_pair(mx_done)
+                mx_done += 1
+            for u, t4, tr in trs:
+                copy_out(tr, u, t4)
+            for T, a2, xt in pend_copy:
+                pend_quant.append((T, a2, x_copy(xt)))
+            pend_copy = []
+            for T, a2 in XDEQ_AT.get(s, ()):
+                pend_copy.append((T, a2, x_widen(T, a2)))
+            for rbit, c in V_AT.get(s, ()):
+                pend_v.append((rbit, c, v_mx(rbit, c)))
+            if s >= 4 and (s - 4) % 2 == 0:
+                u = (s - 4) // 2
+                pq, rbit, ch = UNITS[u]
+                if u >= HALF_FROM:
+                    store(pq, rbit, 4 * ch, 4 * ch + 4)
+                elif ch == 1:
+                    store(pq, rbit, 0, NPOS)

@@ -32,8 +32,8 @@ EV_ON_V = frozenset(((7, 1), (7, 3)))
 V_AT = {0: ((0, 0), (0, 1)), 1: ((0, 2), (0, 3)), 4: ((0, 4), (0, 5)), 5: ((0, 6), (0, 7)), 7: ((1, 0), (1, 1)), 8: ((1, 2), (1, 3)), 10: ((1, 4), (1, 5)), 11: ((1, 6), (1, 7))}
 XDEQ_AT = {0: ((1, 0),), 1: ((1, 1),), 3: ((2, 0),), 4: ((2, 1),), 6: ((3, 0),), 7: ((3, 1),)}
 MX_LEAD = 1
-V_HALF = True
-HALF_FROM = 0
+V_HALF = False
+HALF_FROM = 8
 
 
 def tile_hydra_attn_pa_kernel(tc, x_bytes, x_scale, qkv_w, qkv_b, out_0, out_1, out_2):

import math
from contextlib import ExitStack

import concourse.mybir as mybir
from concourse.masks import make_identity

FLOPS = 2 * 2048 * 512 * 1536

F32 = mybir.dt.float32
BF16 = mybir.dt.bfloat16
U32 = mybir.dt.uint32
U8 = mybir.dt.uint8
FP8 = mybir.dt.float8_e4m3fn
FP8X4 = mybir.dt.float8_e4m3fn_x4
ALU = mybir.AluOpType
ACTF = mybir.ActivationFunctionType
AX = mybir.AxisListType

P = 128
NPOS = 8
NFREQ = 8
NH = 16
HD = 32
E = 512
KDIM = 512
CHUNK = 512

UNITS = [(pq, rb, ch) for rb in range(2) for ch in range(2) for pq in range(2)]
NPAIR = 2 * len(UNITS)
P_B_ON_V = frozenset((11, 15))
EV_ON_V = frozenset(((7, 1), (7, 3)))
V_AT = {0: ((0, 0), (0, 1)), 1: ((0, 2), (0, 3)), 4: ((0, 4), (0, 5)), 5: ((0, 6), (0, 7)), 7: ((1, 0), (1, 1)), 8: ((1, 2), (1, 3)), 10: ((1, 4), (1, 5)), 11: ((1, 6), (1, 7))}
XDEQ_AT = {0: ((1, 0),), 1: ((1, 1),), 3: ((2, 0),), 4: ((2, 1),), 6: ((3, 0),), 7: ((3, 1),)}
MX_LEAD = 1
V_HALF = False
HALF_FROM = 8


def tile_hydra_attn_pa_kernel(tc, x_bytes, x_scale, qkv_w, qkv_b, out_0, out_1, out_2):
    nc = tc.nc
    outs = (out_0, out_1, out_2)

    with ExitStack() as ctx:
        const = ctx.enter_context(tc.tile_pool(name="const", bufs=1))
        xwork = ctx.enter_context(tc.tile_pool(name="xwork", bufs=3))
        wwork = ctx.enter_context(tc.tile_pool(name="wwork", bufs=2))
        rot = ctx.enter_context(tc.tile_pool(name="rot", bufs=3))
        psum = ctx.enter_context(tc.psum_pool(name="psum", bufs=8))
        ctx.enter_context(tc.manual_schedule())

        sc = const.tile([P, KDIM], F32, name="sc")
        x_rows = x_bytes.rearrange("b (wi rp rb) (j c) k -> rb (b wi rp) j (c k)", wi=2, rp=4, rb=2, j=2)
        w_rows = qkv_w.rearrange("(p t) n -> p t n", t=4)
        xb = []
        wraw = []
        for T in range(4):
            xb_T = const.tile([P, 4 * KDIM], U8, name="xb%d" % T)
            xb.append(xb_T)
        for part in range(3):
            wraw_p = const.tile([P, 4, E], BF16, name="wraw%d" % part)
            wraw.append(wraw_p)

        def load_x(T):
            nc.sync.dma_start(out=xb[T][:], in_=x_rows[T // 2, :, :, (T % 2) * 2048:(T % 2 + 1) * 2048])

        def load_w(part):
            nc.sync.dma_start(out=wraw[part][:], in_=w_rows[:, :, part * E:(part + 1) * E])

        brow = const.tile([P, P], BF16, name="brow")
        nc.vector.memset(brow[:], 0.0)
        load_x(0)
        nc.sync.dma_start(out=sc[:], in_=x_scale.rearrange("a b c k -> (a b c k)").partition_broadcast(P))
        for q in range(2):
            nc.sync.dma_start(
                out=brow[q * 4:(q + 1) * 4, :].rearrange("p (h i) -> p h i", i=NFREQ),
                in_=qkv_b[q * E:(q + 1) * E].rearrange("(h f i) -> f h i", h=NH, f=4, i=NFREQ),
            )
        load_w(0)
        load_w(1)
        load_w(2)
        bv = const.tile([P, E], BF16, name="bv")
        nc.sync.dma_start(out=bv[:], in_=qkv_b[2 * E:3 * E].partition_broadcast(P))
        load_x(1)
        load_x(2)
        load_x(3)

        ident = const.tile([P, P], F32, name="ident")
        make_identity(nc, ident[:])
        zo = const.tile([P, 2], F32, name="zo")
        nc.vector.memset(zo[:, 0:1], 0.0)
        nc.vector.memset(zo[:, 1:2], 1.0)
        tab = const.tile([P, 2, NPOS, NFREQ], F32, name="tab")
        nc.vector.memset(tab[:, 0, 0, :], 1.0)
        nc.vector.memset(tab[:, 1, 0, :], 0.0)
        for pos in range(1, NPOS):
            for s in range(2):
                for i in range(0, NFREQ, 2):
                    ang = (pos * 10000.0 ** (-i / 8.0), pos * 10000.0 ** (-(i + 1) / 8.0))
                    va = math.cos(ang[0]) if s == 0 else math.sin(ang[0])
                    vb = math.cos(ang[1]) if s == 0 else math.sin(ang[1])
                    dst = tab[:, s, pos, i:i + 2]
                    if s == 0:
                        nc.vector.tensor_scalar(out=dst, in0=zo[:], scalar1=vb - va, scalar2=va, op0=ALU.mult,
                                                op1=ALU.add)
                    else:
                        nc.scalar.activation(out=dst, in_=zo[:], func=ACTF.Copy, bias=va, scale=vb - va)
        perm = const.tile([P, P], F32, name="perm")
        nc.vector.tensor_copy(out=perm[:].rearrange("p (b j r) -> p b j r", b=16, j=2, r=4),
                              in_=ident[:].rearrange("p (b r j) -> p b j r", b=16, r=4, j=2))
        pick = const.tile([P, NFREQ], F32, name="pick")
        nc.vector.tensor_reduce(out=pick[:], in_=ident[:].rearrange("p (h i) -> p i h", i=NFREQ), axis=AX.X, op=ALU.add)
        tabm = const.tile([P, 2 * NPOS, NFREQ], F32, name="tabm")
        nc.vector.tensor_tensor(out=tabm[:], in0=tab[:].rearrange("p s q i -> p (s q) i"),
                                in1=pick[:].unsqueeze(1).to_broadcast([P, 2 * NPOS, NFREQ]), op=ALU.mult)
        cs = const.tile([P, 3 * NPOS], F32, name="cs")
        nc.vector.tensor_reduce(out=cs[:, 0:2 * NPOS], in_=tabm[:], axis=AX.X, op=ALU.add)
        nc.vector.tensor_scalar(out=cs[:, 2 * NPOS:3 * NPOS], in0=cs[:, NPOS:2 * NPOS], scalar1=-1.0, scalar2=None,
                                op0=ALU.mult)
        xc = []
        xs = []
        for T in range(4):
            xc_T = const.tile([P, CHUNK], U32, name="xc%d" % T, align_bytes=64)
            xs_T = const.tile([P, CHUNK], U8, name="xs%d" % T, align_bytes=64)
            xc.append(xc_T)
            xs.append(xs_T)

        def x_widen(T, a2):
            xt = psum.tile([P, 512], F32, name="xt", tag="bank")
            for a in range(2):
                t4 = 2 * a2 + a
                xq = xwork.tile([P, KDIM], BF16, name="xq", bufs=4)
                nc.vector.tensor_tensor(out=xq[:], in0=xb[T][:, t4 * KDIM:(t4 + 1) * KDIM].bitcast(FP8),
                                        in1=sc[:], op=ALU.mult)
                words = xq[:].bitcast(F32)
                for u in range(2):
                    nc.tensor.transpose(xt[:, (2 * a + u) * P:(2 * a + u + 1) * P], words[:, u:256:2], perm[:])
            return xt

        def x_copy(xt):
            xg = xwork.tile([P, 1024], BF16, name="xg", align_bytes=64)
            nc.scalar.copy(out=xg[:].bitcast(F32).rearrange("p (a m u) -> p a m u", a=2, u=2),
                           in_=xt[:].rearrange("p (a u m) -> p a m u", a=2, u=2))
            return xg

        def x_quant(T, a2, xg):
            nc.vector.quantize_mx(out=xc[T][:, a2 * 256:(a2 + 1) * 256].bitcast(FP8X4),
                                  scales=xs[T][:, a2 * 256:(a2 + 1) * 256], in_=xg[:])

        wc = []
        ws = []
        for part in range(3):
            wc_p = const.tile([P, E], U32, name="wc%d" % part, align_bytes=64)
            ws_p = const.tile([P, E], U8, name="ws%d" % part, align_bytes=64)
            wc.append(wc_p)
            ws.append(ws_p)

        def w_lace_qk(part, g, on_act):
            wg = wwork.tile([P, 2 * E], BF16, name="wgh", bufs=4, align_bytes=64)
            src = wraw[part][:].rearrange("p t (h x) -> p h x t", x=HD)
            for half in range(2):
                f = 2 * g + half
                dst = wg[:, half * 512:(half + 1) * 512].rearrange("p (h i t) -> p h i t", h=NH, i=NFREQ, t=4)
                if on_act:
                    nc.scalar.copy(out=dst, in_=src[:, :, f * 8:(f + 1) * 8, :])
                else:
                    nc.gpsimd.tensor_scalar(out=dst, in0=src[:, :, f * 8:(f + 1) * 8, :], scalar1=1.0, scalar2=0.0,
                                            op0=ALU.mult, op1=ALU.add)
            return wg

        def w_quant_qk(part, g, wg):
            nc.vector.quantize_mx(out=wc[part][:, g * 256:(g + 1) * 256].bitcast(FP8X4),
                                  scales=ws[part][:, g * 256:(g + 1) * 256], in_=wg[:])

        def w_lace_v():
            wg = wwork.tile([P, 4 * E], BF16, name="wg", bufs=1, align_bytes=64)
            nc.vector.tensor_copy(out=wg[:].rearrange("p (n t) -> p n t", t=4), in_=wraw[2][:].rearrange("p t n -> p n t"))
            return wg

        def mx(out, lc, ls, rc, rs):
            nc.tensor.matmul_mx(out=out, lhsT=lc.bitcast(FP8X4), lhsT_scale=ls, rhs=rc.bitcast(FP8X4), rhs_scale=rs,
                                start=True, stop=True)

        def pair_of(s):
            pq, rbit, ch = UNITS[s // 2]
            return pq, rbit, ch, 1 - s % 2

        def mx_pair(s):
            pq, rbit, ch, g = pair_of(s)
            T = 2 * rbit + ch
            y = []
            for half in range(2):
                f = 2 * g + half
                y_h = psum.tile([P, 512], F32, name="y%d" % half, tag="bank")
                mx(y_h[:], wc[pq][:, f * P:(f + 1) * P], ws[pq][:, f * P:(f + 1) * P], xc[T][:], xs[T][:])
                y.append(y_h)
            return y

        def views(s):
            pq, rbit, ch, g = pair_of(s)
            if g == 1:
                def yv(t, k):
                    return t[:, k * P:(k + 1) * P]
                return yv, yv, [4 * ch + k for k in range(4)]

            def yr(t, k):
                return t[:].rearrange("p (a w r) -> p r w a", a=4, w=32, r=4)[:, k]

            def sr(t, k):
                return t[:].rearrange("p (w r a) -> p r w a", w=32, r=4, a=4)[:, k]
            return yr, sr, [2 * k + rbit for k in range(4)]

        def first_products(s, y):
            pq, rbit, ch, g = pair_of(s)
            yv, sv, poss = views(s)
            pt = []
            ot = []
            for half in range(2):
                p_h = rot.tile([P, 512], F32, name="p%d%d" % (g, half))
                o_h = rot.tile([P, 512], F32, name="o%d%d" % (g, half))
                pt.append(p_h)
                ot.append(o_h)
            for half in range(2):
                col = pq * 4 + 2 * g + half
                for k in range(4):
                    pos = poss[k]
                    dst = sv(ot[half], k) if pos == 0 else sv(pt[half], k)
                    if half == 1 and s in P_B_ON_V:
                        nc.vector.tensor_scalar(out=dst, in0=yv(y[half], k), scalar1=cs[:, pos:pos + 1],
                                                scalar2=rb[:, col, pos:pos + 1], op0=ALU.mult, op1=ALU.add)
                    else:
                        nc.scalar.activation(out=dst, in_=yv(y[half], k), func=ACTF.Identity,
                                             bias=rb[:, col, pos:pos + 1], scale=cs[:, pos:pos + 1])
            return pt, ot

        def second_products(s, y, pt, ot):
            yv, sv, poss = views(s)
            for half in range(2):
                soff = 2 * NPOS if half == 0 else NPOS
                for k in range(4):
                    pos = poss[k]
                    if pos > 0:
                        nc.vector.scalar_tensor_tensor(out=sv(ot[half], k), in0=yv(y[1 - half], k),
                                                       scalar=cs[:, soff + pos:soff + pos + 1], in1=sv(pt[half], k),
                                                       op0=ALU.mult, op1=ALU.add)

        out_t = []
        for part in range(3):
            out_p = const.tile([P, NH, 2, NPOS, HD], F32, name="out%d" % part)
            out_t.append(out_p)

        def store(part, rbit, c0, c1):
            dst = outs[part].rearrange("w h (rp rb c) d -> rp rb w h c d", rp=4, rb=2, c=8)
            for rp in range(4):
                nc.sync.dma_start(out=dst[rp, rbit, :, :, c0:c1, :].rearrange("w h c d -> w h (c d)"),
                                  in_=out_t[part][rp:P:4, :, rbit, c0:c1, :].rearrange("p h c d -> p h (c d)"))

        def turn_back(o0, o1, t4):
            tr = psum.tile([P, 512], F32, name="tr", tag="bank")
            for half in range(2):
                nc.tensor.transpose(tr[:, half * P:(half + 1) * P], o0[half][:, t4:512:4], ident[:])
            for half in range(2):
                nc.tensor.transpose(tr[:, (2 + half) * P:(3 + half) * P], o1[half][:, t4 * P:(t4 + 1) * P], ident[:])
            return tr

        def copy_out(tr, u, t4):
            pq, rbit, ch = UNITS[u]
            dst = out_t[pq][:, :, rbit, 4 * ch + t4, :].rearrange("p h (f i) -> p h f i", f=4)
            src = tr[:].rearrange("p (f h i) -> p h f i", f=4, h=NH, i=NFREQ)
            if (u, t4) in EV_ON_V:
                nc.vector.tensor_copy(out=dst, in_=src)
            else:
                nc.scalar.copy(out=dst, in_=src)

        def v_mx(rbit, c):
            T = 2 * rbit + c // 4
            t4 = c % 4
            yv_ = psum.tile([P, 512], F32, name="yv_", tag="bank")
            mx(yv_[:], xc[T][:, t4 * P:(t4 + 1) * P], xs[T][:, t4 * P:(t4 + 1) * P], wc[2][:], ws[2][:])
            return yv_

        def v_add(yv_, rbit, c):
            nc.vector.tensor_tensor(out=out_t[2][:, :, rbit, c, :], in0=yv_[:].rearrange("p (h d) -> p h d", d=HD),
                                    in1=bv[:].rearrange("p (h d) -> p h d", d=HD), op=ALU.add)

        wg_q1 = w_lace_qk(0, 1, False)
        wg_k1 = w_lace_qk(1, 1, False)
        wg_k0 = w_lace_qk(1, 0, False)
        xt0 = x_widen(0, 0)
        xt1 = x_widen(0, 1)
        browf = const.tile([P, P], F32, name="browf")
        nc.vector.tensor_copy(out=browf[:], in_=brow[:])
        bps = psum.tile([P, 512], F32, name="bps", tag="bank")
        nc.tensor.transpose(bps[:, 0:P], browf[:], ident[:])
        bT = const.tile([P, 4, 2], F32, name="bT")
        nc.vector.tensor_copy(out=bT[:].rearrange("p a b -> p (a b)"), in_=bps[:, 0:8])
        bS = const.tile([P, 4, 2], F32, name="bS")
        nc.vector.tensor_scalar(out=bS[:, :, 0], in0=bT[:, :, 1], scalar1=-1.0, scalar2=None, op0=ALU.mult)
        nc.vector.tensor_copy(out=bS[:, :, 1], in_=bT[:, :, 0])
        rb = const.tile([P, 8, NPOS], F32, name="rb")
        rb2 = const.tile([P, 8, NPOS], F32, name="rb2")
        nc.vector.tensor_tensor(out=rb2[:], in0=cs[:, 0:NPOS].unsqueeze(1).to_broadcast([P, 8, NPOS]),
                                in1=bT[:].rearrange("p a b -> p (a b)").unsqueeze(2).to_broadcast([P, 8, NPOS]), op=ALU.mult)
        nc.vector.tensor_tensor(out=rb[:], in0=cs[:, NPOS:2 * NPOS].unsqueeze(1).to_broadcast([P, 8, NPOS]),
                                in1=bS[:].rearrange("p a b -> p (a b)").unsqueeze(2).to_broadcast([P, 8, NPOS]), op=ALU.mult)
        nc.vector.tensor_tensor(out=rb[:], in0=rb[:], in1=rb2[:], op=ALU.add)

        xg0 = x_copy(xt0)
        xg1 = x_copy(xt1)
        wg_q0 = w_lace_qk(0, 0, True)
        x_quant(0, 0, xg0)
        w_quant_qk(0, 1, wg_q1)
        x_quant(0, 1, xg1)
        w_quant_qk(0, 0, wg_q0)
        ys = {}
        ys[0] = mx_pair(0)
        ys[1] = mx_pair(1)
        mx_done = 2
        wg_v = w_lace_v()
        w_quant_qk(1, 1, wg_k1)
        nc.vector.quantize_mx(out=wc[2][:].bitcast(FP8X4), scales=ws[2][:], in_=wg_v[:])
        w_quant_qk(1, 0, wg_k0)
        pend_copy = []
        pend_quant = []
        chunk_ready = {0: 2, 1: 0, 2: 0, 3: 0}
        pend_v = []
        v_count = {0: 0, 1: 0}
        ps_ = {}
        os_ = {}
        k_quant = False

        for s in range(NPAIR + 3):
            if 1 <= s <= NPAIR:
                second_products(s - 1, ys[s - 1], ps_[s - 1], os_[s - 1])
            for rbit, c, yv_ in pend_v:
                v_add(yv_, rbit, c)
                v_count[rbit] += 1
                if V_HALF and v_count[rbit] % 4 == 0:
                    store(2, rbit, v_count[rbit] - 4, v_count[rbit])
                elif v_count[rbit] == NPOS:
                    store(2, rbit, 0, NPOS)
            pend_v = []
            trs = []
            if s >= 3:
                u = (s - 3) // 2
                for t4 in ((0, 1) if (s - 3) % 2 == 0 else (2, 3)):
                    trs.append((u, t4, turn_back(os_[2 * u + 1], os_[2 * u], t4)))
            if s < NPAIR:
                ps_[s], os_[s] = first_products(s, ys[s])
            for T, a2, xg in pend_quant:
                x_quant(T, a2, xg)
                chunk_ready[T] += 1
            pend_quant = []
            while mx_done < NPAIR and mx_done <= s + MX_LEAD:
                npq, nrb, nch, ng = pair_of(mx_done)
                if chunk_ready[2 * nrb + nch] < 2:
                    break
                ys[mx_done] = mx_pair(mx_done)
                mx_done += 1
            for u, t4, tr in trs:
                copy_out(tr, u, t4)
            for T, a2, xt in pend_copy:
                pend_quant.append((T, a2, x_copy(xt)))
            pend_copy = []
            for T, a2 in XDEQ_AT.get(s, ()):
                pend_copy.append((T, a2, x_widen(T, a2)))
            for rbit, c in V_AT.get(s, ()):
                pend_v.append((rbit, c, v_mx(rbit, c)))
            if s >= 4 and (s - 4) % 2 == 0:
                u = (s - 4) // 2
                pq, rbit, ch = UNITS[u]
                if u >= HALF_FROM:
                    store(pq, rbit, 4 * ch, 4 * ch + 4)
                elif ch == 1:
                    store(pq, rbit, 0, NPOS)
